import numpy as np
import ml_dtypes


def mxq(x, axis, fmt="e4m3"):
    dtype, down = {"e4m3": (ml_dtypes.float8_e4m3fn, 7), "e5m2": (ml_dtypes.float8_e5m2, 14)}[fmt]
    v = np.moveaxis(np.asarray(x, np.float32).astype(ml_dtypes.bfloat16).astype(np.float64), axis, -1)
    blocks = v.reshape(v.shape[:-1] + (-1, 32))
    amax = np.abs(blocks).max(-1, keepdims=True)
    byte = np.maximum(np.where(amax > 0, np.frexp(amax)[1] - 1 + 127, 0) - down, 1)
    scale = np.exp2(byte - 127.0)
    codes = (blocks / scale).astype(np.float32).astype(dtype).astype(np.float64)
    return np.moveaxis((codes * scale).reshape(v.shape), -1, axis)


WIDE = False


def mx_kscale(k):
    if not WIDE:
        return np.ones(k)
    levels = np.array([10, -10, 5, -5, 0])
    a = np.random.permutation(np.resize(levels, k // 512 * 4)).reshape(k // 512, 4)
    idx = np.arange(k)
    return np.exp2(a[idx // 512, idx % 128 // 32])


BF16 = ml_dtypes.bfloat16


def bf(x):
    return np.asarray(x, np.float32).astype(BF16)


def f64(x):
    return np.asarray(x).astype(np.float64)


B, S, D, P, PW, L = 4, 2048, 512, 4, 2, 2


def sigmoid(v):
    return 1.0 / (1.0 + np.exp(-v))


def setup_inputs():
    n = np.random.standard_normal
    s = mx_kscale(D)
    return {"x": bf(n((B, S, D)) * s),
            "amp_w": bf(n((D, D)) / np.sqrt(D) / s[:, None]),
            "amp_b": bf(n(D) * 0.3),
            "ph_w": bf(n((D, D)) / np.sqrt(D) / s[:, None]),
            "ph_b": bf(n(D) * 0.3)}


def reference(x, amp_w, amp_b, ph_w, ph_b):
    xq = mxq(f64(x), 2, "e4m3")
    amp = sigmoid((xq @ mxq(f64(amp_w), 0, "e4m3")) + f64(amp_b))
    ph = np.tanh((xq @ mxq(f64(ph_w), 0, "e4m3")) + f64(ph_b)) * np.pi
    return (np.cos(ph) + np.sin(ph)) * amp

@@ -1,0 +1,205 @@
+import math
+from contextlib import ExitStack
+
+import concourse.mybir as mybir
+from concourse.masks import make_identity
+
+F32 = mybir.dt.float32
+BF16 = mybir.dt.bfloat16
+U32 = mybir.dt.uint32
+U8 = mybir.dt.uint8
+FP8X4 = mybir.dt.float8_e4m3fn_x4
+ACT = mybir.ActivationFunctionType
+ALU = mybir.AluOpType
+
+P = 128
+PACK = 4
+K = P * PACK
+FEATURES = 512
+BLOCKS = FEATURES // P
+TOKENS = 4 * 2048
+CHUNK = 512
+TILES = CHUNK // P
+CHUNKS = TOKENS // CHUNK
+STEPS = CHUNKS * BLOCKS
+assert TILES == BLOCKS
+
+X_LEAD = 6
+W_LEAD = 1
+LAG = 5
+
+FLOPS = 2 * TOKENS * K * 2 * FEATURES
+
+
+def tile_quantuminspiredneuralcore_pa_t_kernel(tc, x, amp_w, amp_b, ph_w, ph_b, out):
+    nc = tc.nc
+    x_chunks = x.flatten_outer_dims().rearrange("(c p r) k -> c p r k", p=P, r=TILES)
+    out_tiles = out.flatten_outer_dims().rearrange("(c p r) f -> c r p f", p=P, r=TILES)
+    weights = {"amp": amp_w, "ph": ph_w}
+
+    with ExitStack() as stack:
+        keep = stack.enter_context(tc.tile_pool(name="keep", bufs=1))
+        stage = stack.enter_context(tc.tile_pool(name="stage", bufs=3))
+        psum_mx = stack.enter_context(tc.psum_pool(name="psum_mx", bufs=3))
+        psum_ph = stack.enter_context(tc.psum_pool(name="psum_ph", bufs=2))
+        psum_amp = stack.enter_context(tc.psum_pool(name="psum_amp", bufs=2))
+        psum_x = stack.enter_context(tc.psum_pool(name="psum_x", bufs=1))
+        stack.enter_context(tc.manual_schedule())
+
+        x_all = keep.tile([P, CHUNKS, TILES, K], BF16)
+        x_words = x_all[:].bitcast(F32)
+        bias_rows = keep.tile([2 * BLOCKS, P], BF16)
+        w_raw = {}
+        nc.sync.dma_start(out=x_all[:, 0], in_=x_chunks[0])
+        nc.scalar.dma_start(out=bias_rows[0:BLOCKS, :], in_=amp_b.rearrange("(j f) -> j f", f=P))
+        nc.scalar.dma_start(out=bias_rows[BLOCKS : 2 * BLOCKS, :], in_=ph_b.rearrange("(j f) -> j f", f=P))
+        for branch in ("amp", "ph"):
+            w_raw[branch] = keep.tile([P, PACK, FEATURES], BF16, name="w_raw_" + branch)
+            for u in range(2):
+                nc.scalar.dma_start(
+                    out=w_raw[branch][:, 2 * u : 2 * u + 2, :],
+                    in_=weights[branch][2 * P * u : 2 * P * (u + 1), :].rearrange("(q e) f -> q e f", e=2),
+                )
+        for c in range(1, CHUNKS):
+            nc.sync.dma_start(out=x_all[:, c], in_=x_chunks[c])
+
+        ident = keep.tile([P, P], F32)
+        make_identity(nc, ident[:])
+        ones = keep.tile([P, 1], F32)
+        nc.vector.memset(ones[:], 1.0)
+        table_pick = keep.tile([P, 1], F32)
+        nc.scalar.activation(out=table_pick[:], in_=ones[:], func=ACT.Silu)
+        phase = keep.tile([P, 1], F32)
+        nc.vector.tensor_scalar_mul(out=phase[:], in0=ones[:], scalar1=3.0 * math.pi / 8.0)
+
+        bias_square = keep.tile([P, P], F32)
+        nc.vector.memset(bias_square[:], 0.0)
+        nc.vector.tensor_copy(out=bias_square[0 : 2 * BLOCKS, :], in_=bias_rows[:])
+        bias_t = psum_x.tile([P, 2, P], F32, tag="x_t")
+        nc.tensor.transpose(bias_t[:, 0, :], bias_square[:], ident[:])
+        bias = {"amp": keep.tile([P, BLOCKS], F32, name="bias_amp"), "ph": keep.tile([P, BLOCKS], F32, name="bias_ph")}
+        nc.vector.tensor_scalar_mul(out=bias["amp"][:], in0=bias_t[:, 0, 0:BLOCKS], scalar1=0.5)
+        nc.vector.tensor_copy(out=bias["ph"][:], in_=bias_t[:, 0, BLOCKS : 2 * BLOCKS])
+        tanh_scale = {"amp": 0.5, "ph": 1.0}
+
+        w_grouped = {}
+        w_codes = {}
+        w_scales = {}
+        for branch in ("amp", "ph"):
+            w_grouped[branch] = keep.tile([P, FEATURES, PACK], BF16, align_bytes=64, name="w_grouped_" + branch)
+            w_codes[branch] = keep.tile([P, FEATURES], U32, align_bytes=64, name="w_codes_" + branch)
+            w_scales[branch] = keep.tile([P, FEATURES], U8, align_bytes=64, name="w_scales_" + branch)
+
+        def quantise_weight_block(j):
+            feats = slice(j * P, (j + 1) * P)
+            for branch in ("amp", "ph"):
+                nc.vector.tensor_copy(
+                    out=w_grouped[branch][:, feats, :],
+                    in_=w_raw[branch][:, :, feats].rearrange("p t f -> p f t"),
+                )
+            for branch in ("amp", "ph"):
+                nc.vector.quantize_mx(
+                    out=w_codes[branch][:, feats].bitcast(FP8X4),
+                    scales=w_scales[branch][:, feats],
+                    in_=w_grouped[branch][:, feats, :].rearrange("p f t -> p (f t)"),
+                )
+
+        x_grouped = {}
+        x_codes = {}
+        x_scales = {}
+
+        def transpose_tokens(tile_no):
+            c, r = divmod(tile_no, TILES)
+            x_t = psum_x.tile([P, 2, P], F32, tag="x_t")
+            for u in range(2):
+                nc.tensor.transpose(x_t[:, u, :], x_words[:, c, r, u * P : (u + 1) * P], ident[:])
+            x_grouped[tile_no] = stage.tile([P, P * PACK], BF16, align_bytes=64, name="x_grouped")
+            nc.vector.tensor_copy(
+                out=x_grouped[tile_no][:].bitcast(F32).rearrange("p (n u) -> p n u", u=2),
+                in_=x_t[:].rearrange("p u n -> p n u"),
+            )
+
+        def quantise_tokens(tile_no):
+            c, r = divmod(tile_no, TILES)
+            if r == 0:
+                x_codes[c] = stage.tile([P, CHUNK], U32, align_bytes=64, name="x_codes")
+                x_scales[c] = stage.tile([P, CHUNK], U8, align_bytes=64, name="x_scales")
+            toks = slice(r * P, (r + 1) * P)
+            nc.vector.quantize_mx(
+                out=x_codes[c][:, toks].bitcast(FP8X4),
+                scales=x_scales[c][:, toks],
+                in_=x_grouped[tile_no][:],
+            )
+
+        tanh = {}
+
+        def project(step):
+            c, j = divmod(step, BLOCKS)
+            feats = slice(j * P, (j + 1) * P)
+            if j == 0:
+                tanh["amp", c] = stage.tile([P, BLOCKS, CHUNK], F32, name="tanh_amp")
+                tanh["ph", c] = stage.tile([P, BLOCKS, CHUNK], F32, name="tanh_ph")
+            product = {}
+            for branch in ("amp", "ph"):
+                product[branch] = psum_mx.tile([P, CHUNK], F32, name="product")
+                nc.tensor.matmul_mx(
+                    out=product[branch][:],
+                    lhsT=w_codes[branch][:, feats].bitcast(FP8X4),
+                    lhsT_scale=w_scales[branch][:, feats],
+                    rhs=x_codes[c][:].bitcast(FP8X4),
+                    rhs_scale=x_scales[c][:],
+                    start=True,
+                    stop=True,
+                )
+            for branch in ("amp", "ph"):
+                nc.scalar.activation(
+                    out=tanh[branch, c][:, j, :],
+                    in_=product[branch][:],
+                    func=ACT.Tanh,
+                    bias=bias[branch][:, j : j + 1],
+                    scale=tanh_scale[branch],
+                )
+
+        def amplitude(step):
+            c, j = divmod(step, BLOCKS)
+            nc.vector.tensor_scalar(
+                out=tanh["amp", c][:, j, :],
+                in0=tanh["amp", c][:, j, :],
+                scalar1=math.sqrt(2.0),
+                scalar2=math.sqrt(2.0),
+                op0=ALU.mult,
+                op1=ALU.add,
+            )
+
+        def finish(tile_no):
+            c, r = divmod(tile_no, TILES)
+            toks = slice(r * P, (r + 1) * P)
+            ph_t = psum_ph.tile([P, FEATURES], F32)
+            amp_t = psum_amp.tile([P, FEATURES], F32)
+            for j in range(BLOCKS):
+                nc.tensor.transpose(ph_t[:, j * P : (j + 1) * P], tanh["ph", c][:, j, toks], ident[:])
+            for j in range(BLOCKS):
+                nc.tensor.transpose(amp_t[:, j * P : (j + 1) * P], tanh["amp", c][:, j, toks], ident[:])
+            half_cos = stage.tile([P, FEATURES], F32)
+            nc.scalar.activation(out=half_cos[:], in_=ph_t[:], func=ACT.Sin, bias=phase[:], scale=math.pi / 2.0)
+            square = stage.tile([P, FEATURES], F32)
+            nc.vector.tensor_mul(out=square[:], in0=half_cos[:], in1=half_cos[:])
+            result = stage.tile([P, FEATURES], F32)
+            nc.vector.scalar_tensor_tensor(
+                out=result[:], in0=square[:], scalar=-0.5, in1=amp_t[:], op0=ALU.add, op1=ALU.mult
+            )
+            nc.sync.dma_start(out=out_tiles[c, r], in_=result[:])
+
+        for step in range(-X_LEAD, STEPS + LAG):
+            if 0 <= step < STEPS:
+                project(step)
+            if 0 <= step - 1 < STEPS:
+                amplitude(step - 1)
+            if 0 <= step + X_LEAD < STEPS:
+                transpose_tokens(step + X_LEAD)
+            if 0 <= step + X_LEAD - 1 < STEPS:
+                quantise_tokens(step + X_LEAD - 1)
+            if 0 <= step + W_LEAD < BLOCKS:
+                quantise_weight_block(step + W_LEAD)
+            if 0 <= step - LAG < STEPS:
+                finish(step - LAG)

@@ -42,8 +42,7 @@ def tile_quantuminspiredneuralcore_pa_t_kernel(tc, x, amp_w, amp_b, ph_w, ph_b, 
         stage = stack.enter_context(tc.tile_pool(name="stage", bufs=3))
         psum_mx = stack.enter_context(tc.psum_pool(name="psum_mx", bufs=3))
         psum_ph = stack.enter_context(tc.psum_pool(name="psum_ph", bufs=2))
-        psum_amp = stack.enter_context(tc.psum_pool(name="psum_amp", bufs=2))
-        psum_x = stack.enter_context(tc.psum_pool(name="psum_x", bufs=1))
+        psum_v = stack.enter_context(tc.psum_pool(name="psum_v", bufs=3))
         stack.enter_context(tc.manual_schedule())
 
         x_all = keep.tile([P, CHUNKS, TILES, K], BF16)
@@ -75,7 +74,7 @@ def tile_quantuminspiredneuralcore_pa_t_kernel(tc, x, amp_w, amp_b, ph_w, ph_b, 
         bias_square = keep.tile([P, P], F32)
         nc.vector.memset(bias_square[:], 0.0)
         nc.vector.tensor_copy(out=bias_square[0 : 2 * BLOCKS, :], in_=bias_rows[:])
-        bias_t = psum_x.tile([P, 2, P], F32, tag="x_t")
+        bias_t = psum_v.tile([P, 2, P], F32, tag="for_vector")
         nc.tensor.transpose(bias_t[:, 0, :], bias_square[:], ident[:])
         bias = {"amp": keep.tile([P, BLOCKS], F32, name="bias_amp"), "ph": keep.tile([P, BLOCKS], F32, name="bias_ph")}
         nc.vector.tensor_scalar_mul(out=bias["amp"][:], in0=bias_t[:, 0, 0:BLOCKS], scalar1=0.5)
@@ -110,7 +109,7 @@ def tile_quantuminspiredneuralcore_pa_t_kernel(tc, x, amp_w, amp_b, ph_w, ph_b, 
 
         def transpose_tokens(tile_no):
             c, r = divmod(tile_no, TILES)
-            x_t = psum_x.tile([P, 2, P], F32, tag="x_t")
+            x_t = psum_v.tile([P, 2, P], F32, tag="for_vector")
             for u in range(2):
                 nc.tensor.transpose(x_t[:, u, :], x_words[:, c, r, u * P : (u + 1) * P], ident[:])
             x_grouped[tile_no] = stage.tile([P, P * PACK], BF16, align_bytes=64, name="x_grouped")
@@ -162,7 +161,7 @@ def tile_quantuminspiredneuralcore_pa_t_kernel(tc, x, amp_w, amp_b, ph_w, ph_b, 
 
         def amplitude(step):
             c, j = divmod(step, BLOCKS)
-            nc.vector.tensor_scalar(
+            nc.gpsimd.tensor_scalar(
                 out=tanh["amp", c][:, j, :],
                 in0=tanh["amp", c][:, j, :],
                 scalar1=math.sqrt(2.0),
@@ -171,35 +170,47 @@ def tile_quantuminspiredneuralcore_pa_t_kernel(tc, x, amp_w, amp_b, ph_w, ph_b, 
                 op1=ALU.add,
             )
 
-        def finish(tile_no):
+        amp_t = {}
+        square = {}
+
+        def turn_back(tile_no):
             c, r = divmod(tile_no, TILES)
             toks = slice(r * P, (r + 1) * P)
             ph_t = psum_ph.tile([P, FEATURES], F32)
-            amp_t = psum_amp.tile([P, FEATURES], F32)
+            amp_t[tile_no] = psum_v.tile([P, FEATURES], F32, name="amp_t", tag="for_vector")
             for j in range(BLOCKS):
                 nc.tensor.transpose(ph_t[:, j * P : (j + 1) * P], tanh["ph", c][:, j, toks], ident[:])
             for j in range(BLOCKS):
-                nc.tensor.transpose(amp_t[:, j * P : (j + 1) * P], tanh["amp", c][:, j, toks], ident[:])
+                nc.tensor.transpose(amp_t[tile_no][:, j * P : (j + 1) * P], tanh["amp", c][:, j, toks], ident[:])
             half_cos = stage.tile([P, FEATURES], F32)
             nc.scalar.activation(out=half_cos[:], in_=ph_t[:], func=ACT.Sin, bias=phase[:], scale=math.pi / 2.0)
-            square = stage.tile([P, FEATURES], F32)
-            nc.vector.tensor_mul(out=square[:], in0=half_cos[:], in1=half_cos[:])
+            square[tile_no] = stage.tile([P, FEATURES], F32, name="square")
+            nc.vector.tensor_mul(out=square[tile_no][:], in0=half_cos[:], in1=half_cos[:])
+
+        def combine(tile_no):
+            c, r = divmod(tile_no, TILES)
             result = stage.tile([P, FEATURES], F32)
             nc.vector.scalar_tensor_tensor(
-                out=result[:], in0=square[:], scalar=-0.5, in1=amp_t[:], op0=ALU.add, op1=ALU.mult
+                out=result[:],
+                in0=square[tile_no][:],
+                scalar=-0.5,
+                in1=amp_t[tile_no][:],
+                op0=ALU.add,
+                op1=ALU.mult,
             )
             nc.sync.dma_start(out=out_tiles[c, r], in_=result[:])
 
         for step in range(-X_LEAD, STEPS + LAG):
             if 0 <= step < STEPS:
                 project(step)
-            if 0 <= step - 1 < STEPS:
-                amplitude(step - 1)
-            if 0 <= step + X_LEAD < STEPS:
-                transpose_tokens(step + X_LEAD)
+                amplitude(step)
+            if 0 <= step - LAG < STEPS:
+                turn_back(step - LAG)
             if 0 <= step + X_LEAD - 1 < STEPS:
                 quantise_tokens(step + X_LEAD - 1)
+            if 0 <= step + X_LEAD < STEPS:
+                transpose_tokens(step + X_LEAD)
             if 0 <= step + W_LEAD < BLOCKS:
                 quantise_weight_block(step + W_LEAD)
             if 0 <= step - LAG < STEPS:
-                finish(step - LAG)
+                combine(step - LAG)

@@ -42,7 +42,8 @@ def tile_quantuminspiredneuralcore_pa_t_kernel(tc, x, amp_w, amp_b, ph_w, ph_b, 
         stage = stack.enter_context(tc.tile_pool(name="stage", bufs=3))
         psum_mx = stack.enter_context(tc.psum_pool(name="psum_mx", bufs=3))
         psum_ph = stack.enter_context(tc.psum_pool(name="psum_ph", bufs=2))
-        psum_v = stack.enter_context(tc.psum_pool(name="psum_v", bufs=3))
+        psum_amp = stack.enter_context(tc.psum_pool(name="psum_amp", bufs=2))
+        psum_x = stack.enter_context(tc.psum_pool(name="psum_x", bufs=1))
         stack.enter_context(tc.manual_schedule())
 
         x_all = keep.tile([P, CHUNKS, TILES, K], BF16)
@@ -74,7 +75,7 @@ def tile_quantuminspiredneuralcore_pa_t_kernel(tc, x, amp_w, amp_b, ph_w, ph_b, 
         bias_square = keep.tile([P, P], F32)
         nc.vector.memset(bias_square[:], 0.0)
         nc.vector.tensor_copy(out=bias_square[0 : 2 * BLOCKS, :], in_=bias_rows[:])
-        bias_t = psum_v.tile([P, 2, P], F32, tag="for_vector")
+        bias_t = psum_x.tile([P, 2, P], F32, tag="bank")
         nc.tensor.transpose(bias_t[:, 0, :], bias_square[:], ident[:])
         bias = {"amp": keep.tile([P, BLOCKS], F32, name="bias_amp"), "ph": keep.tile([P, BLOCKS], F32, name="bias_ph")}
         nc.vector.tensor_scalar_mul(out=bias["amp"][:], in0=bias_t[:, 0, 0:BLOCKS], scalar1=0.5)
@@ -107,9 +108,9 @@ def tile_quantuminspiredneuralcore_pa_t_kernel(tc, x, amp_w, amp_b, ph_w, ph_b, 
         x_codes = {}
         x_scales = {}
 
-        def transpose_tokens(tile_no):
+        def transpose_tokens(tile_no, banks):
             c, r = divmod(tile_no, TILES)
-            x_t = psum_v.tile([P, 2, P], F32, tag="for_vector")
+            x_t = banks.tile([P, 2, P], F32, tag="bank")
             for u in range(2):
                 nc.tensor.transpose(x_t[:, u, :], x_words[:, c, r, u * P : (u + 1) * P], ident[:])
             x_grouped[tile_no] = stage.tile([P, P * PACK], BF16, align_bytes=64, name="x_grouped")
@@ -140,7 +141,7 @@ def tile_quantuminspiredneuralcore_pa_t_kernel(tc, x, amp_w, amp_b, ph_w, ph_b, 
                 tanh["ph", c] = stage.tile([P, BLOCKS, CHUNK], F32, name="tanh_ph")
             product = {}
             for branch in ("amp", "ph"):
-                product[branch] = psum_mx.tile([P, CHUNK], F32, name="product")
+                product[branch] = psum_mx.tile([P, CHUNK], F32, name="product", tag="bank")
                 nc.tensor.matmul_mx(
                     out=product[branch][:],
                     lhsT=w_codes[branch][:, feats].bitcast(FP8X4),
@@ -170,47 +171,49 @@ def tile_quantuminspiredneuralcore_pa_t_kernel(tc, x, amp_w, amp_b, ph_w, ph_b, 
                 op1=ALU.add,
             )
 
-        amp_t = {}
+        half_cos = {}
         square = {}
 
-        def turn_back(tile_no):
+        def turn_phase_back(tile_no):
             c, r = divmod(tile_no, TILES)
             toks = slice(r * P, (r + 1) * P)
             ph_t = psum_ph.tile([P, FEATURES], F32)
-            amp_t[tile_no] = psum_v.tile([P, FEATURES], F32, name="amp_t", tag="for_vector")
             for j in range(BLOCKS):
                 nc.tensor.transpose(ph_t[:, j * P : (j + 1) * P], tanh["ph", c][:, j, toks], ident[:])
-            for j in range(BLOCKS):
-                nc.tensor.transpose(amp_t[tile_no][:, j * P : (j + 1) * P], tanh["amp", c][:, j, toks], ident[:])
-            half_cos = stage.tile([P, FEATURES], F32)
-            nc.scalar.activation(out=half_cos[:], in_=ph_t[:], func=ACT.Sin, bias=phase[:], scale=math.pi / 2.0)
+            half_cos[tile_no] = stage.tile([P, FEATURES], F32, name="half_cos")
+            nc.scalar.activation(
+                out=half_cos[tile_no][:], in_=ph_t[:], func=ACT.Sin, bias=phase[:], scale=math.pi / 2.0
+            )
+
+        def square_half_cos(tile_no):
             square[tile_no] = stage.tile([P, FEATURES], F32, name="square")
-            nc.vector.tensor_mul(out=square[tile_no][:], in0=half_cos[:], in1=half_cos[:])
+            nc.vector.tensor_mul(out=square[tile_no][:], in0=half_cos[tile_no][:], in1=half_cos[tile_no][:])
 
         def combine(tile_no):
             c, r = divmod(tile_no, TILES)
+            toks = slice(r * P, (r + 1) * P)
+            amp_t = psum_amp.tile([P, FEATURES], F32)
+            for j in range(BLOCKS):
+                nc.tensor.transpose(amp_t[:, j * P : (j + 1) * P], tanh["amp", c][:, j, toks], ident[:])
             result = stage.tile([P, FEATURES], F32)
             nc.vector.scalar_tensor_tensor(
-                out=result[:],
-                in0=square[tile_no][:],
-                scalar=-0.5,
-                in1=amp_t[tile_no][:],
-                op0=ALU.add,
-                op1=ALU.mult,
+                out=result[:], in0=square[tile_no][:], scalar=-0.5, in1=amp_t[:], op0=ALU.add, op1=ALU.mult
             )
             nc.sync.dma_start(out=out_tiles[c, r], in_=result[:])
 
-        for step in range(-X_LEAD, STEPS + LAG):
+        for step in range(-X_LEAD, STEPS + LAG + 1):
             if 0 <= step < STEPS:
                 project(step)
                 amplitude(step)
             if 0 <= step - LAG < STEPS:
-                turn_back(step - LAG)
+                turn_phase_back(step - LAG)
+            if 0 <= step - LAG - 1 < STEPS:
+                combine(step - LAG - 1)
+            if 0 <= step - LAG < STEPS:
+                square_half_cos(step - LAG)
             if 0 <= step + X_LEAD - 1 < STEPS:
                 quantise_tokens(step + X_LEAD - 1)
             if 0 <= step + X_LEAD < STEPS:
-                transpose_tokens(step + X_LEAD)
+                transpose_tokens(step + X_LEAD, psum_mx if step < 0 else psum_x)
             if 0 <= step + W_LEAD < BLOCKS:
                 quantise_weight_block(step + W_LEAD)
-            if 0 <= step - LAG < STEPS:
-                combine(step - LAG)

@@ -25,8 +25,9 @@ STEPS = CHUNKS * BLOCKS
 assert TILES == BLOCKS
 
 X_LEAD = 6
-W_LEAD = 1
-LAG = 5
+W_LEAD = 2
+LAG = 4
+MULTIPLY_LAG = LAG + 2
 
 FLOPS = 2 * TOKENS * K * 2 * FEATURES
 
@@ -201,19 +202,19 @@ def tile_quantuminspiredneuralcore_pa_t_kernel(tc, x, amp_w, amp_b, ph_w, ph_b, 
             )
             nc.sync.dma_start(out=out_tiles[c, r], in_=result[:])
 
-        for step in range(-X_LEAD, STEPS + LAG + 1):
+        for step in range(-X_LEAD, STEPS + MULTIPLY_LAG):
             if 0 <= step < STEPS:
                 project(step)
                 amplitude(step)
             if 0 <= step - LAG < STEPS:
                 turn_phase_back(step - LAG)
-            if 0 <= step - LAG - 1 < STEPS:
-                combine(step - LAG - 1)
-            if 0 <= step - LAG < STEPS:
-                square_half_cos(step - LAG)
             if 0 <= step + X_LEAD - 1 < STEPS:
                 quantise_tokens(step + X_LEAD - 1)
+            if 0 <= step - MULTIPLY_LAG < STEPS:
+                combine(step - MULTIPLY_LAG)
             if 0 <= step + X_LEAD < STEPS:
                 transpose_tokens(step + X_LEAD, psum_mx if step < 0 else psum_x)
             if 0 <= step + W_LEAD < BLOCKS:
                 quantise_weight_block(step + W_LEAD)
+            if 0 <= step - LAG < STEPS:
+                square_half_cos(step - LAG)

@@ -208,12 +208,12 @@ def tile_quantuminspiredneuralcore_pa_t_kernel(tc, x, amp_w, amp_b, ph_w, ph_b, 
                 amplitude(step)
             if 0 <= step - LAG < STEPS:
                 turn_phase_back(step - LAG)
-            if 0 <= step + X_LEAD - 1 < STEPS:
-                quantise_tokens(step + X_LEAD - 1)
             if 0 <= step - MULTIPLY_LAG < STEPS:
                 combine(step - MULTIPLY_LAG)
             if 0 <= step + X_LEAD < STEPS:
                 transpose_tokens(step + X_LEAD, psum_mx if step < 0 else psum_x)
+            if 0 <= step + X_LEAD - 1 < STEPS:
+                quantise_tokens(step + X_LEAD - 1)
             if 0 <= step + W_LEAD < BLOCKS:
                 quantise_weight_block(step + W_LEAD)
             if 0 <= step - LAG < STEPS:

@@ -22,25 +22,30 @@ CHUNK = 512
 TILES = CHUNK // P
 CHUNKS = TOKENS // CHUNK
 STEPS = CHUNKS * BLOCKS
-assert TILES == BLOCKS
+PAIRS = CHUNKS * 2
+PAIR_TOKENS = 2 * P
 
+LAG_H = 2
+LAG_A = LAG_H + 2
 X_LEAD = 6
-W_LEAD = 2
-LAG = 4
-MULTIPLY_LAG = LAG + 2
+LOADS_AHEAD = 4
 
 FLOPS = 2 * TOKENS * K * 2 * FEATURES
 
 
 def tile_quantuminspiredneuralcore_pa_t_kernel(tc, x, amp_w, amp_b, ph_w, ph_b, out):
     nc = tc.nc
-    x_chunks = x.flatten_outer_dims().rearrange("(c p r) k -> c p r k", p=P, r=TILES)
-    out_tiles = out.flatten_outer_dims().rearrange("(c p r) f -> c r p f", p=P, r=TILES)
+    x_rows = x.flatten_outer_dims()
+    x_pairs = x_rows.rearrange("(c p h i) k -> c h p i k", p=P, h=2, i=2)
+    x_chunks = x_rows.rearrange("(c p r) k -> c p r k", p=P, r=TILES)
+    out_blocks = out.flatten_outer_dims().rearrange("(c p r) (j f) -> c j p r f", p=P, r=TILES, f=P)
     weights = {"amp": amp_w, "ph": ph_w}
+    branches = ("amp", "ph")
 
     with ExitStack() as stack:
         keep = stack.enter_context(tc.tile_pool(name="keep", bufs=1))
-        stage = stack.enter_context(tc.tile_pool(name="stage", bufs=3))
+        stage = stack.enter_context(tc.tile_pool(name="stage", bufs=4))
+        deep = stack.enter_context(tc.tile_pool(name="deep", bufs=6))
         psum_mx = stack.enter_context(tc.psum_pool(name="psum_mx", bufs=3))
         psum_ph = stack.enter_context(tc.psum_pool(name="psum_ph", bufs=2))
         psum_amp = stack.enter_context(tc.psum_pool(name="psum_amp", bufs=2))
@@ -51,17 +56,27 @@ def tile_quantuminspiredneuralcore_pa_t_kernel(tc, x, amp_w, amp_b, ph_w, ph_b, 
         x_words = x_all[:].bitcast(F32)
         bias_rows = keep.tile([2 * BLOCKS, P], BF16)
         w_raw = {}
-        nc.sync.dma_start(out=x_all[:, 0], in_=x_chunks[0])
+        for branch in branches:
+            w_raw[branch] = keep.tile([P, PACK, FEATURES], BF16, name="w_raw_" + branch)
+
+        def load_weights(branch, half):
+            feats = slice(half * 2 * P, (half + 1) * 2 * P)
+            for u in range(2):
+                nc.sync.dma_start(
+                    out=w_raw[branch][:, 2 * u : 2 * u + 2, feats],
+                    in_=weights[branch][2 * P * u : 2 * P * (u + 1), feats].rearrange("(q e) f -> q e f", e=2),
+                )
+
         nc.scalar.dma_start(out=bias_rows[0:BLOCKS, :], in_=amp_b.rearrange("(j f) -> j f", f=P))
         nc.scalar.dma_start(out=bias_rows[BLOCKS : 2 * BLOCKS, :], in_=ph_b.rearrange("(j f) -> j f", f=P))
-        for branch in ("amp", "ph"):
-            w_raw[branch] = keep.tile([P, PACK, FEATURES], BF16, name="w_raw_" + branch)
-            for u in range(2):
-                nc.scalar.dma_start(
-                    out=w_raw[branch][:, 2 * u : 2 * u + 2, :],
-                    in_=weights[branch][2 * P * u : 2 * P * (u + 1), :].rearrange("(q e) f -> q e f", e=2),
-                )
-        for c in range(1, CHUNKS):
+        nc.sync.dma_start(out=x_all[:, 0, 0:2], in_=x_pairs[0, 0])
+        load_weights("amp", 0)
+        nc.sync.dma_start(out=x_all[:, 0, 2:4], in_=x_pairs[0, 1])
+        load_weights("ph", 0)
+        nc.sync.dma_start(out=x_all[:, 1], in_=x_chunks[1])
+        load_weights("amp", 1)
+        load_weights("ph", 1)
+        for c in range(2, LOADS_AHEAD):
             nc.sync.dma_start(out=x_all[:, c], in_=x_chunks[c])
 
         ident = keep.tile([P, P], F32)
@@ -76,60 +91,67 @@ def tile_quantuminspiredneuralcore_pa_t_kernel(tc, x, amp_w, amp_b, ph_w, ph_b, 
         bias_square = keep.tile([P, P], F32)
         nc.vector.memset(bias_square[:], 0.0)
         nc.vector.tensor_copy(out=bias_square[0 : 2 * BLOCKS, :], in_=bias_rows[:])
-        bias_t = psum_x.tile([P, 2, P], F32, tag="bank")
-        nc.tensor.transpose(bias_t[:, 0, :], bias_square[:], ident[:])
+        bias_t = psum_x.tile([P, 2, 2, P], F32, tag="bank")
+        nc.tensor.transpose(bias_t[:, 0, 0, :], bias_square[:], ident[:])
         bias = {"amp": keep.tile([P, BLOCKS], F32, name="bias_amp"), "ph": keep.tile([P, BLOCKS], F32, name="bias_ph")}
-        nc.vector.tensor_scalar_mul(out=bias["amp"][:], in0=bias_t[:, 0, 0:BLOCKS], scalar1=0.5)
-        nc.vector.tensor_copy(out=bias["ph"][:], in_=bias_t[:, 0, BLOCKS : 2 * BLOCKS])
+        nc.vector.tensor_scalar_mul(out=bias["amp"][:], in0=bias_t[:, 0, 0, 0:BLOCKS], scalar1=0.5)
+        nc.vector.tensor_copy(out=bias["ph"][:], in_=bias_t[:, 0, 0, BLOCKS : 2 * BLOCKS])
         tanh_scale = {"amp": 0.5, "ph": 1.0}
 
         w_grouped = {}
         w_codes = {}
         w_scales = {}
-        for branch in ("amp", "ph"):
+        for branch in branches:
             w_grouped[branch] = keep.tile([P, FEATURES, PACK], BF16, align_bytes=64, name="w_grouped_" + branch)
             w_codes[branch] = keep.tile([P, FEATURES], U32, align_bytes=64, name="w_codes_" + branch)
             w_scales[branch] = keep.tile([P, FEATURES], U8, align_bytes=64, name="w_scales_" + branch)
 
-        def quantise_weight_block(j):
+        def group_weights(branch, j):
             feats = slice(j * P, (j + 1) * P)
-            for branch in ("amp", "ph"):
-                nc.vector.tensor_copy(
-                    out=w_grouped[branch][:, feats, :],
-                    in_=w_raw[branch][:, :, feats].rearrange("p t f -> p f t"),
-                )
-            for branch in ("amp", "ph"):
-                nc.vector.quantize_mx(
-                    out=w_codes[branch][:, feats].bitcast(FP8X4),
-                    scales=w_scales[branch][:, feats],
-                    in_=w_grouped[branch][:, feats, :].rearrange("p f t -> p (f t)"),
-                )
+            nc.vector.tensor_copy(
+                out=w_grouped[branch][:, feats, :],
+                in_=w_raw[branch][:, :, feats].rearrange("p t f -> p f t"),
+            )
 
+        def quantise_weights(branch, j):
+            feats = slice(j * P, (j + 1) * P)
+            nc.vector.quantize_mx(
+                out=w_codes[branch][:, feats].bitcast(FP8X4),
+                scales=w_scales[branch][:, feats],
+                in_=w_grouped[branch][:, feats, :].rearrange("p f t -> p (f t)"),
+            )
+
+        x_t = {}
         x_grouped = {}
         x_codes = {}
         x_scales = {}
 
-        def transpose_tokens(tile_no, banks):
-            c, r = divmod(tile_no, TILES)
-            x_t = banks.tile([P, 2, P], F32, tag="bank")
-            for u in range(2):
-                nc.tensor.transpose(x_t[:, u, :], x_words[:, c, r, u * P : (u + 1) * P], ident[:])
-            x_grouped[tile_no] = stage.tile([P, P * PACK], BF16, align_bytes=64, name="x_grouped")
-            nc.vector.tensor_copy(
-                out=x_grouped[tile_no][:].bitcast(F32).rearrange("p (n u) -> p n u", u=2),
-                in_=x_t[:].rearrange("p u n -> p n u"),
-            )
+        def transpose_pair(e, banks):
+            c, h = divmod(e, 2)
+            x_t[e] = banks.tile([P, 2, 2, P], F32, tag="bank", name="x_t")
+            for i in range(2):
+                for u in range(2):
+                    nc.tensor.transpose(x_t[e][:, i, u, :], x_words[:, c, 2 * h + i, u * P : (u + 1) * P], ident[:])
 
-        def quantise_tokens(tile_no):
-            c, r = divmod(tile_no, TILES)
-            if r == 0:
+        def copy_pair(e, on_scalar):
+            x_grouped[e] = stage.tile([P, PAIR_TOKENS * PACK], BF16, align_bytes=64, name="x_grouped")
+            dst = x_grouped[e][:].bitcast(F32).rearrange("p (i n u) -> p i n u", i=2, u=2)
+            src = x_t[e][:].rearrange("p i u n -> p i n u")
+            if on_scalar:
+                nc.scalar.copy(out=dst, in_=src)
+            else:
+                nc.vector.tensor_copy(out=dst, in_=src)
+
+        def quantise_pair(e):
+            c, h = divmod(e, 2)
+            if h == 0:
                 x_codes[c] = stage.tile([P, CHUNK], U32, align_bytes=64, name="x_codes")
                 x_scales[c] = stage.tile([P, CHUNK], U8, align_bytes=64, name="x_scales")
-            toks = slice(r * P, (r + 1) * P)
+            toks = slice(h * PAIR_TOKENS, (h + 1) * PAIR_TOKENS)
             nc.vector.quantize_mx(
                 out=x_codes[c][:, toks].bitcast(FP8X4),
                 scales=x_scales[c][:, toks],
-                in_=x_grouped[tile_no][:],
+                in_=x_grouped[e][:],
             )
 
         tanh = {}
@@ -137,11 +159,8 @@ def tile_quantuminspiredneuralcore_pa_t_kernel(tc, x, amp_w, amp_b, ph_w, ph_b, 
         def project(step):
             c, j = divmod(step, BLOCKS)
             feats = slice(j * P, (j + 1) * P)
-            if j == 0:
-                tanh["amp", c] = stage.tile([P, BLOCKS, CHUNK], F32, name="tanh_amp")
-                tanh["ph", c] = stage.tile([P, BLOCKS, CHUNK], F32, name="tanh_ph")
             product = {}
-            for branch in ("amp", "ph"):
+            for branch in branches:
                 product[branch] = psum_mx.tile([P, CHUNK], F32, name="product", tag="bank")
                 nc.tensor.matmul_mx(
                     out=product[branch][:],
@@ -152,9 +171,10 @@ def tile_quantuminspiredneuralcore_pa_t_kernel(tc, x, amp_w, amp_b, ph_w, ph_b, 
                     start=True,
                     stop=True,
                 )
-            for branch in ("amp", "ph"):
+            for branch in branches:
+                tanh[branch, step] = deep.tile([P, CHUNK], F32, name="tanh_" + branch)
                 nc.scalar.activation(
-                    out=tanh[branch, c][:, j, :],
+                    out=tanh[branch, step][:],
                     in_=product[branch][:],
                     func=ACT.Tanh,
                     bias=bias[branch][:, j : j + 1],
@@ -162,10 +182,9 @@ def tile_quantuminspiredneuralcore_pa_t_kernel(tc, x, amp_w, amp_b, ph_w, ph_b, 
                 )
 
         def amplitude(step):
-            c, j = divmod(step, BLOCKS)
             nc.gpsimd.tensor_scalar(
-                out=tanh["amp", c][:, j, :],
-                in0=tanh["amp", c][:, j, :],
+                out=tanh["amp", step][:],
+                in0=tanh["amp", step][:],
                 scalar1=math.sqrt(2.0),
                 scalar2=math.sqrt(2.0),
                 op0=ALU.mult,
@@ -175,46 +194,69 @@ def tile_quantuminspiredneuralcore_pa_t_kernel(tc, x, amp_w, amp_b, ph_w, ph_b, 
         half_cos = {}
         square = {}
 
-        def turn_phase_back(tile_no):
-            c, r = divmod(tile_no, TILES)
-            toks = slice(r * P, (r + 1) * P)
-            ph_t = psum_ph.tile([P, FEATURES], F32)
-            for j in range(BLOCKS):
-                nc.tensor.transpose(ph_t[:, j * P : (j + 1) * P], tanh["ph", c][:, j, toks], ident[:])
-            half_cos[tile_no] = stage.tile([P, FEATURES], F32, name="half_cos")
-            nc.scalar.activation(
-                out=half_cos[tile_no][:], in_=ph_t[:], func=ACT.Sin, bias=phase[:], scale=math.pi / 2.0
-            )
+        def turn_back(bank, source):
+            for r in range(TILES):
+                toks = slice(r * P, (r + 1) * P)
+                nc.tensor.transpose(bank[:, toks], source[:, toks], ident[:])
 
-        def square_half_cos(tile_no):
-            square[tile_no] = stage.tile([P, FEATURES], F32, name="square")
-            nc.vector.tensor_mul(out=square[tile_no][:], in0=half_cos[tile_no][:], in1=half_cos[tile_no][:])
+        def phase_back(step):
+            ph_t = psum_ph.tile([P, CHUNK], F32)
+            turn_back(ph_t, tanh["ph", step])
+            half_cos[step] = stage.tile([P, CHUNK], F32, name="half_cos")
+            nc.scalar.activation(out=half_cos[step][:], in_=ph_t[:], func=ACT.Sin, bias=phase[:], scale=math.pi / 2.0)
 
-        def combine(tile_no):
-            c, r = divmod(tile_no, TILES)
-            toks = slice(r * P, (r + 1) * P)
-            amp_t = psum_amp.tile([P, FEATURES], F32)
-            for j in range(BLOCKS):
-                nc.tensor.transpose(amp_t[:, j * P : (j + 1) * P], tanh["amp", c][:, j, toks], ident[:])
-            result = stage.tile([P, FEATURES], F32)
+        def square_half_cos(step):
+            square[step] = stage.tile([P, CHUNK], F32, name="square")
+            nc.vector.tensor_mul(out=square[step][:], in0=half_cos[step][:], in1=half_cos[step][:])
+
+        def combine(step):
+            c, j = divmod(step, BLOCKS)
+            amp_t = psum_amp.tile([P, CHUNK], F32)
+            turn_back(amp_t, tanh["amp", step])
+            result = stage.tile([P, CHUNK], F32)
             nc.vector.scalar_tensor_tensor(
-                out=result[:], in0=square[tile_no][:], scalar=-0.5, in1=amp_t[:], op0=ALU.add, op1=ALU.mult
+                out=result[:], in0=square[step][:], scalar=-0.5, in1=amp_t[:], op0=ALU.add, op1=ALU.mult
             )
-            nc.sync.dma_start(out=out_tiles[c, r], in_=result[:])
+            nc.sync.dma_start(out=out_blocks[c, j], in_=result[:].rearrange("p (r f) -> p r f", f=P))
 
-        for step in range(-X_LEAD, STEPS + MULTIPLY_LAG):
-            if 0 <= step < STEPS:
+        group_weights("amp", 0)
+        transpose_pair(0, psum_mx)
+        copy_pair(0, False)
+        quantise_weights("amp", 0)
+        transpose_pair(1, psum_mx)
+        copy_pair(1, True)
+        quantise_pair(0)
+        group_weights("ph", 0)
+        quantise_pair(1)
+        quantise_weights("ph", 0)
+
+        pair_step = {2: 0, 3: 1}
+        for e in range(4, PAIRS):
+            pair_step[e] = 2 * e - X_LEAD
+        pairs_at = {}
+        for e in pair_step:
+            pairs_at[pair_step[e]] = e
+
+        for step in range(0, STEPS + LAG_A):
+            if step % BLOCKS == 0 and step // BLOCKS + LOADS_AHEAD < CHUNKS:
+                nc.sync.dma_start(out=x_all[:, step // BLOCKS + LOADS_AHEAD], in_=x_chunks[step // BLOCKS + LOADS_AHEAD])
+            if step < STEPS:
                 project(step)
                 amplitude(step)
-            if 0 <= step - LAG < STEPS:
-                turn_phase_back(step - LAG)
-            if 0 <= step - MULTIPLY_LAG < STEPS:
-                combine(step - MULTIPLY_LAG)
-            if 0 <= step + X_LEAD < STEPS:
-                transpose_tokens(step + X_LEAD, psum_mx if step < 0 else psum_x)
-            if 0 <= step + X_LEAD - 1 < STEPS:
-                quantise_tokens(step + X_LEAD - 1)
-            if 0 <= step + W_LEAD < BLOCKS:
-                quantise_weight_block(step + W_LEAD)
-            if 0 <= step - LAG < STEPS:
-                square_half_cos(step - LAG)
+            if 0 <= step - LAG_H < STEPS:
+                phase_back(step - LAG_H)
+            if 0 <= step - LAG_A < STEPS:
+                combine(step - LAG_A)
+            if step + 1 < BLOCKS:
+                for branch in branches:
+                    group_weights(branch, step + 1)
+            if step in pairs_at:
+                transpose_pair(pairs_at[step], psum_x)
+                copy_pair(pairs_at[step], False)
+            if step + 1 < BLOCKS:
+                for branch in branches:
+                    quantise_weights(branch, step + 1)
+            if step - 1 in pairs_at:
+                quantise_pair(pairs_at[step - 1])
+            if 0 <= step - LAG_H < STEPS:
+                square_half_cos(step - LAG_H)

@@ -28,6 +28,7 @@ PAIR_TOKENS = 2 * P
 LAG_H = 2
 LAG_A = LAG_H + 2
 X_LEAD = 6
+TAIL_FROM = STEPS - 2
 LOADS_AHEAD = 4
 
 FLOPS = 2 * TOKENS * K * 2 * FEATURES
@@ -70,8 +71,8 @@ def tile_quantuminspiredneuralcore_pa_t_kernel(tc, x, amp_w, amp_b, ph_w, ph_b, 
         nc.scalar.dma_start(out=bias_rows[0:BLOCKS, :], in_=amp_b.rearrange("(j f) -> j f", f=P))
         nc.scalar.dma_start(out=bias_rows[BLOCKS : 2 * BLOCKS, :], in_=ph_b.rearrange("(j f) -> j f", f=P))
         nc.sync.dma_start(out=x_all[:, 0, 0:2], in_=x_pairs[0, 0])
-        load_weights("amp", 0)
         nc.sync.dma_start(out=x_all[:, 0, 2:4], in_=x_pairs[0, 1])
+        load_weights("amp", 0)
         load_weights("ph", 0)
         nc.sync.dma_start(out=x_all[:, 1], in_=x_chunks[1])
         load_weights("amp", 1)
@@ -154,32 +155,33 @@ def tile_quantuminspiredneuralcore_pa_t_kernel(tc, x, amp_w, amp_b, ph_w, ph_b, 
                 in_=x_grouped[e][:],
             )
 
+        product = {}
         tanh = {}
 
-        def project(step):
+        def multiply(step, branch):
             c, j = divmod(step, BLOCKS)
             feats = slice(j * P, (j + 1) * P)
-            product = {}
-            for branch in branches:
-                product[branch] = psum_mx.tile([P, CHUNK], F32, name="product", tag="bank")
-                nc.tensor.matmul_mx(
-                    out=product[branch][:],
-                    lhsT=w_codes[branch][:, feats].bitcast(FP8X4),
-                    lhsT_scale=w_scales[branch][:, feats],
-                    rhs=x_codes[c][:].bitcast(FP8X4),
-                    rhs_scale=x_scales[c][:],
-                    start=True,
-                    stop=True,
-                )
-            for branch in branches:
-                tanh[branch, step] = deep.tile([P, CHUNK], F32, name="tanh_" + branch)
-                nc.scalar.activation(
-                    out=tanh[branch, step][:],
-                    in_=product[branch][:],
-                    func=ACT.Tanh,
-                    bias=bias[branch][:, j : j + 1],
-                    scale=tanh_scale[branch],
-                )
+            product[branch, step] = psum_mx.tile([P, CHUNK], F32, name="product", tag="bank")
+            nc.tensor.matmul_mx(
+                out=product[branch, step][:],
+                lhsT=w_codes[branch][:, feats].bitcast(FP8X4),
+                lhsT_scale=w_scales[branch][:, feats],
+                rhs=x_codes[c][:].bitcast(FP8X4),
+                rhs_scale=x_scales[c][:],
+                start=True,
+                stop=True,
+            )
+
+        def squash(step, branch):
+            j = step % BLOCKS
+            tanh[branch, step] = deep.tile([P, CHUNK], F32, name="tanh_" + branch)
+            nc.scalar.activation(
+                out=tanh[branch, step][:],
+                in_=product[branch, step][:],
+                func=ACT.Tanh,
+                bias=bias[branch][:, j : j + 1],
+                scale=tanh_scale[branch],
+            )
 
         def amplitude(step):
             nc.gpsimd.tensor_scalar(
@@ -191,6 +193,8 @@ def tile_quantuminspiredneuralcore_pa_t_kernel(tc, x, amp_w, amp_b, ph_w, ph_b, 
                 op1=ALU.add,
             )
 
+        ph_t = {}
+        amp_t = {}
         half_cos = {}
         square = {}
 
@@ -200,35 +204,47 @@ def tile_quantuminspiredneuralcore_pa_t_kernel(tc, x, amp_w, amp_b, ph_w, ph_b, 
                 nc.tensor.transpose(bank[:, toks], source[:, toks], ident[:])
 
         def phase_back(step):
-            ph_t = psum_ph.tile([P, CHUNK], F32)
-            turn_back(ph_t, tanh["ph", step])
-            half_cos[step] = stage.tile([P, CHUNK], F32, name="half_cos")
-            nc.scalar.activation(out=half_cos[step][:], in_=ph_t[:], func=ACT.Sin, bias=phase[:], scale=math.pi / 2.0)
+            ph_t[step] = psum_ph.tile([P, CHUNK], F32, name="ph_t")
+            turn_back(ph_t[step], tanh["ph", step])
 
-        def square_half_cos(step):
+        def sine(step):
+            half_cos[step] = stage.tile([P, CHUNK], F32, name="half_cos")
+            nc.scalar.activation(
+                out=half_cos[step][:], in_=ph_t[step][:], func=ACT.Sin, bias=phase[:], scale=math.pi / 2.0
+            )
+
+        def square_half_cos(step, on_scalar):
             square[step] = stage.tile([P, CHUNK], F32, name="square")
-            nc.vector.tensor_mul(out=square[step][:], in0=half_cos[step][:], in1=half_cos[step][:])
+            if on_scalar:
+                nc.scalar.activation(out=square[step][:], in_=half_cos[step][:], func=ACT.Square)
+            else:
+                nc.vector.tensor_mul(out=square[step][:], in0=half_cos[step][:], in1=half_cos[step][:])
+
+        def amp_back(step):
+            amp_t[step] = psum_amp.tile([P, CHUNK], F32, name="amp_t")
+            turn_back(amp_t[step], tanh["amp", step])
 
         def combine(step):
             c, j = divmod(step, BLOCKS)
-            amp_t = psum_amp.tile([P, CHUNK], F32)
-            turn_back(amp_t, tanh["amp", step])
             result = stage.tile([P, CHUNK], F32)
             nc.vector.scalar_tensor_tensor(
-                out=result[:], in0=square[step][:], scalar=-0.5, in1=amp_t[:], op0=ALU.add, op1=ALU.mult
+                out=result[:], in0=square[step][:], scalar=-0.5, in1=amp_t[step][:], op0=ALU.add, op1=ALU.mult
             )
             nc.sync.dma_start(out=out_blocks[c, j], in_=result[:].rearrange("p (r f) -> p r f", f=P))
 
-        group_weights("amp", 0)
         transpose_pair(0, psum_mx)
         copy_pair(0, False)
-        quantise_weights("amp", 0)
         transpose_pair(1, psum_mx)
         copy_pair(1, True)
+        group_weights("amp", 0)
         quantise_pair(0)
-        group_weights("ph", 0)
+        quantise_weights("amp", 0)
         quantise_pair(1)
+        group_weights("ph", 0)
+        group_weights("amp", 1)
         quantise_weights("ph", 0)
+        group_weights("ph", 1)
+        quantise_weights("amp", 1)
 
         pair_step = {2: 0, 3: 1}
         for e in range(4, PAIRS):
@@ -237,26 +253,67 @@ def tile_quantuminspiredneuralcore_pa_t_kernel(tc, x, amp_w, amp_b, ph_w, ph_b, 
         for e in pair_step:
             pairs_at[pair_step[e]] = e
 
-        for step in range(0, STEPS + LAG_A):
+        for step in range(0, TAIL_FROM):
             if step % BLOCKS == 0 and step // BLOCKS + LOADS_AHEAD < CHUNKS:
                 nc.sync.dma_start(out=x_all[:, step // BLOCKS + LOADS_AHEAD], in_=x_chunks[step // BLOCKS + LOADS_AHEAD])
-            if step < STEPS:
-                project(step)
-                amplitude(step)
-            if 0 <= step - LAG_H < STEPS:
+            for branch in branches:
+                multiply(step, branch)
+            for branch in branches:
+                squash(step, branch)
+            amplitude(step)
+            if step >= LAG_H:
                 phase_back(step - LAG_H)
-            if 0 <= step - LAG_A < STEPS:
+                sine(step - LAG_H)
+            if step >= LAG_A:
+                amp_back(step - LAG_A)
                 combine(step - LAG_A)
-            if step + 1 < BLOCKS:
+            if step == 0:
+                quantise_weights("ph", 1)
+            if 1 <= step < BLOCKS - 1:
                 for branch in branches:
                     group_weights(branch, step + 1)
+                for branch in branches:
+                    quantise_weights(branch, step + 1)
             if step in pairs_at:
                 transpose_pair(pairs_at[step], psum_x)
                 copy_pair(pairs_at[step], False)
-            if step + 1 < BLOCKS:
-                for branch in branches:
-                    quantise_weights(branch, step + 1)
             if step - 1 in pairs_at:
                 quantise_pair(pairs_at[step - 1])
-            if 0 <= step - LAG_H < STEPS:
-                square_half_cos(step - LAG_H)
+            if step >= LAG_H:
+                square_half_cos(step - LAG_H, False)
+
+        a, b = TAIL_FROM, TAIL_FROM + 1
+        multiply(a, "ph")
+        multiply(a, "amp")
+        phase_back(a - 2)
+        squash(a, "ph")
+        sine(a - 2)
+        squash(a, "amp")
+        amplitude(a)
+        amp_back(a - 4)
+        combine(a - 4)
+        square_half_cos(a - 2, False)
+        phase_back(a - 1)
+        multiply(b, "ph")
+        multiply(b, "amp")
+        sine(a - 1)
+        squash(b, "ph")
+        amp_back(a - 3)
+        combine(a - 3)
+        square_half_cos(a - 1, False)
+        phase_back(a)
+        sine(a)
+        squash(b, "amp")
+        amplitude(b)
+        amp_back(a - 2)
+        combine(a - 2)
+        square_half_cos(a, False)
+        phase_back(b)
+        sine(b)
+        amp_back(a - 1)
+        combine(a - 1)
+        square_half_cos(b, True)
+        amp_back(a)
+        combine(a)
+        amp_back(b)
+        combine(b)

@@ -29,6 +29,8 @@ LAG_H = 2
 LAG_A = LAG_H + 2
 X_LEAD = 6
 TAIL_FROM = STEPS - 2
+WARM_BEFORE = 4
+WARM_AFTER = 4
 LOADS_AHEAD = 4
 
 FLOPS = 2 * TOKENS * K * 2 * FEATURES
@@ -80,6 +82,15 @@ def tile_quantuminspiredneuralcore_pa_t_kernel(tc, x, amp_w, amp_b, ph_w, ph_b, 
         for c in range(2, LOADS_AHEAD):
             nc.sync.dma_start(out=x_all[:, c], in_=x_chunks[c])
 
+        zeros = keep.tile([P, CHUNK], BF16)
+        nc.vector.memset(zeros[:], 0.0)
+
+        def warm_up(passes):
+            idle = psum_amp.tile([P, CHUNK], F32, name="amp_t")
+            for i in range(passes):
+                nc.tensor.matmul(out=idle[:], lhsT=zeros[:, 0:P], rhs=zeros[:], start=True, stop=True)
+
+        warm_up(WARM_BEFORE)
         ident = keep.tile([P, P], F32)
         make_identity(nc, ident[:])
         ones = keep.tile([P, 1], F32)
@@ -91,12 +102,7 @@ def tile_quantuminspiredneuralcore_pa_t_kernel(tc, x, amp_w, amp_b, ph_w, ph_b, 
 
         bias_square = keep.tile([P, P], F32)
         nc.vector.memset(bias_square[:], 0.0)
-        nc.vector.tensor_copy(out=bias_square[0 : 2 * BLOCKS, :], in_=bias_rows[:])
-        bias_t = psum_x.tile([P, 2, 2, P], F32, tag="bank")
-        nc.tensor.transpose(bias_t[:, 0, 0, :], bias_square[:], ident[:])
         bias = {"amp": keep.tile([P, BLOCKS], F32, name="bias_amp"), "ph": keep.tile([P, BLOCKS], F32, name="bias_ph")}
-        nc.vector.tensor_scalar_mul(out=bias["amp"][:], in0=bias_t[:, 0, 0, 0:BLOCKS], scalar1=0.5)
-        nc.vector.tensor_copy(out=bias["ph"][:], in_=bias_t[:, 0, 0, BLOCKS : 2 * BLOCKS])
         tanh_scale = {"amp": 0.5, "ph": 1.0}
 
         w_grouped = {}
@@ -236,9 +242,15 @@ def tile_quantuminspiredneuralcore_pa_t_kernel(tc, x, amp_w, amp_b, ph_w, ph_b, 
         copy_pair(0, False)
         transpose_pair(1, psum_mx)
         copy_pair(1, True)
+        nc.vector.tensor_copy(out=bias_square[0 : 2 * BLOCKS, :], in_=bias_rows[:])
+        bias_t = psum_x.tile([P, 2, 2, P], F32, tag="bank")
+        nc.tensor.transpose(bias_t[:, 0, 0, :], bias_square[:], ident[:])
+        warm_up(WARM_AFTER)
         group_weights("amp", 0)
         quantise_pair(0)
         quantise_weights("amp", 0)
+        nc.vector.tensor_scalar_mul(out=bias["amp"][:], in0=bias_t[:, 0, 0, 0:BLOCKS], scalar1=0.5)
+        nc.vector.tensor_copy(out=bias["ph"][:], in_=bias_t[:, 0, 0, BLOCKS : 2 * BLOCKS])
         quantise_pair(1)
         group_weights("ph", 0)
         group_weights("amp", 1)

@@ -97,8 +97,6 @@ def tile_quantuminspiredneuralcore_pa_t_kernel(tc, x, amp_w, amp_b, ph_w, ph_b, 
         nc.vector.memset(ones[:], 1.0)
         table_pick = keep.tile([P, 1], F32)
         nc.scalar.activation(out=table_pick[:], in_=ones[:], func=ACT.Silu)
-        phase = keep.tile([P, 1], F32)
-        nc.vector.tensor_scalar_mul(out=phase[:], in0=ones[:], scalar1=3.0 * math.pi / 8.0)
 
         bias_square = keep.tile([P, P], F32)
         nc.vector.memset(bias_square[:], 0.0)
@@ -216,7 +214,7 @@ def tile_quantuminspiredneuralcore_pa_t_kernel(tc, x, amp_w, amp_b, ph_w, ph_b, 
         def sine(step):
             half_cos[step] = stage.tile([P, CHUNK], F32, name="half_cos")
             nc.scalar.activation(
-                out=half_cos[step][:], in_=ph_t[step][:], func=ACT.Sin, bias=phase[:], scale=math.pi / 2.0
+                out=half_cos[step][:], in_=ph_t[step][:], func=ACT.Sin, bias=3.0 * math.pi / 8.0, scale=math.pi / 2.0
             )
 
         def square_half_cos(step, on_scalar):

import math
from contextlib import ExitStack

import concourse.mybir as mybir
from concourse.masks import make_identity

F32 = mybir.dt.float32
BF16 = mybir.dt.bfloat16
U32 = mybir.dt.uint32
U8 = mybir.dt.uint8
FP8X4 = mybir.dt.float8_e4m3fn_x4
ACT = mybir.ActivationFunctionType
ALU = mybir.AluOpType

P = 128
PACK = 4
K = P * PACK
FEATURES = 512
BLOCKS = FEATURES // P
TOKENS = 4 * 2048
CHUNK = 512
TILES = CHUNK // P
CHUNKS = TOKENS // CHUNK
STEPS = CHUNKS * BLOCKS
PAIRS = CHUNKS * 2
PAIR_TOKENS = 2 * P

LAG_H = 2
LAG_A = LAG_H + 2
X_LEAD = 6
TAIL_FROM = STEPS - 2
WARM_BEFORE = 4
WARM_AFTER = 4
LOADS_AHEAD = 4

FLOPS = 2 * TOKENS * K * 2 * FEATURES


def tile_quantuminspiredneuralcore_pa_t_kernel(tc, x, amp_w, amp_b, ph_w, ph_b, out):
    nc = tc.nc
    x_rows = x.flatten_outer_dims()
    x_pairs = x_rows.rearrange("(c p h i) k -> c h p i k", p=P, h=2, i=2)
    x_chunks = x_rows.rearrange("(c p r) k -> c p r k", p=P, r=TILES)
    out_blocks = out.flatten_outer_dims().rearrange("(c p r) (j f) -> c j p r f", p=P, r=TILES, f=P)
    weights = {"amp": amp_w, "ph": ph_w}
    branches = ("amp", "ph")

    with ExitStack() as stack:
        keep = stack.enter_context(tc.tile_pool(name="keep", bufs=1))
        stage = stack.enter_context(tc.tile_pool(name="stage", bufs=4))
        deep = stack.enter_context(tc.tile_pool(name="deep", bufs=6))
        psum_mx = stack.enter_context(tc.psum_pool(name="psum_mx", bufs=3))
        psum_ph = stack.enter_context(tc.psum_pool(name="psum_ph", bufs=2))
        psum_amp = stack.enter_context(tc.psum_pool(name="psum_amp", bufs=2))
        psum_x = stack.enter_context(tc.psum_pool(name="psum_x", bufs=1))
        stack.enter_context(tc.manual_schedule())

        x_all = keep.tile([P, CHUNKS, TILES, K], BF16)
        x_words = x_all[:].bitcast(F32)
        bias_rows = keep.tile([2 * BLOCKS, P], BF16)
        w_raw = {}
        for branch in branches:
            w_raw[branch] = keep.tile([P, PACK, FEATURES], BF16, name="w_raw_" + branch)

        def load_weights(branch, half):
            feats = slice(half * 2 * P, (half + 1) * 2 * P)
            for u in range(2):
                nc.sync.dma_start(
                    out=w_raw[branch][:, 2 * u : 2 * u + 2, feats],
                    in_=weights[branch][2 * P * u : 2 * P * (u + 1), feats].rearrange("(q e) f -> q e f", e=2),
                )

        nc.scalar.dma_start(out=bias_rows[0:BLOCKS, :], in_=amp_b.rearrange("(j f) -> j f", f=P))
        nc.scalar.dma_start(out=bias_rows[BLOCKS : 2 * BLOCKS, :], in_=ph_b.rearrange("(j f) -> j f", f=P))
        nc.sync.dma_start(out=x_all[:, 0, 0:2], in_=x_pairs[0, 0])
        nc.sync.dma_start(out=x_all[:, 0, 2:4], in_=x_pairs[0, 1])
        load_weights("amp", 0)
        load_weights("ph", 0)
        nc.sync.dma_start(out=x_all[:, 1], in_=x_chunks[1])
        load_weights("amp", 1)
        load_weights("ph", 1)
        for c in range(2, LOADS_AHEAD):
            nc.sync.dma_start(out=x_all[:, c], in_=x_chunks[c])

        zeros = keep.tile([P, CHUNK], BF16)
        nc.vector.memset(zeros[:], 0.0)

        def warm_up(passes):
            idle = psum_amp.tile([P, CHUNK], F32, name="amp_t")
            for i in range(passes):
                nc.tensor.matmul(out=idle[:], lhsT=zeros[:, 0:P], rhs=zeros[:], start=True, stop=True)

        warm_up(WARM_BEFORE)
        ident = keep.tile([P, P], F32)
        make_identity(nc, ident[:])
        ones = keep.tile([P, 1], F32)
        nc.vector.memset(ones[:], 1.0)
        table_pick = keep.tile([P, 1], F32)
        nc.scalar.activation(out=table_pick[:], in_=ones[:], func=ACT.Silu)

        bias_square = keep.tile([P, P], F32)
        nc.vector.memset(bias_square[:], 0.0)
        bias = {"amp": keep.tile([P, BLOCKS], F32, name="bias_amp"), "ph": keep.tile([P, BLOCKS], F32, name="bias_ph")}
        tanh_scale = {"amp": 0.5, "ph": 1.0}

        w_grouped = {}
        w_codes = {}
        w_scales = {}
        for branch in branches:
            w_grouped[branch] = keep.tile([P, FEATURES, PACK], BF16, align_bytes=64, name="w_grouped_" + branch)
            w_codes[branch] = keep.tile([P, FEATURES], U32, align_bytes=64, name="w_codes_" + branch)
            w_scales[branch] = keep.tile([P, FEATURES], U8, align_bytes=64, name="w_scales_" + branch)

        def group_weights(branch, j):
            feats = slice(j * P, (j + 1) * P)
            nc.vector.tensor_copy(
                out=w_grouped[branch][:, feats, :],
                in_=w_raw[branch][:, :, feats].rearrange("p t f -> p f t"),
            )

        def quantise_weights(branch, j):
            feats = slice(j * P, (j + 1) * P)
            nc.vector.quantize_mx(
                out=w_codes[branch][:, feats].bitcast(FP8X4),
                scales=w_scales[branch][:, feats],
                in_=w_grouped[branch][:, feats, :].rearrange("p f t -> p (f t)"),
            )

        x_t = {}
        x_grouped = {}
        x_codes = {}
        x_scales = {}

        def transpose_pair(e, banks):
            c, h = divmod(e, 2)
            x_t[e] = banks.tile([P, 2, 2, P], F32, tag="bank", name="x_t")
            for i in range(2):
                for u in range(2):
                    nc.tensor.transpose(x_t[e][:, i, u, :], x_words[:, c, 2 * h + i, u * P : (u + 1) * P], ident[:])

        def copy_pair(e, on_scalar):
            x_grouped[e] = stage.tile([P, PAIR_TOKENS * PACK], BF16, align_bytes=64, name="x_grouped")
            dst = x_grouped[e][:].bitcast(F32).rearrange("p (i n u) -> p i n u", i=2, u=2)
            src = x_t[e][:].rearrange("p i u n -> p i n u")
            if on_scalar:
                nc.scalar.copy(out=dst, in_=src)
            else:
                nc.vector.tensor_copy(out=dst, in_=src)

        def quantise_pair(e):
            c, h = divmod(e, 2)
            if h == 0:
                x_codes[c] = stage.tile([P, CHUNK], U32, align_bytes=64, name="x_codes")
                x_scales[c] = stage.tile([P, CHUNK], U8, align_bytes=64, name="x_scales")
            toks = slice(h * PAIR_TOKENS, (h + 1) * PAIR_TOKENS)
            nc.vector.quantize_mx(
                out=x_codes[c][:, toks].bitcast(FP8X4),
                scales=x_scales[c][:, toks],
                in_=x_grouped[e][:],
            )

        product = {}
        tanh = {}

        def multiply(step, branch):
            c, j = divmod(step, BLOCKS)
            feats = slice(j * P, (j + 1) * P)
            product[branch, step] = psum_mx.tile([P, CHUNK], F32, name="product", tag="bank")
            nc.tensor.matmul_mx(
                out=product[branch, step][:],
                lhsT=w_codes[branch][:, feats].bitcast(FP8X4),
                lhsT_scale=w_scales[branch][:, feats],
                rhs=x_codes[c][:].bitcast(FP8X4),
                rhs_scale=x_scales[c][:],
                start=True,
                stop=True,
            )

        def squash(step, branch):
            j = step % BLOCKS
            tanh[branch, step] = deep.tile([P, CHUNK], F32, name="tanh_" + branch)
            nc.scalar.activation(
                out=tanh[branch, step][:],
                in_=product[branch, step][:],
                func=ACT.Tanh,
                bias=bias[branch][:, j : j + 1],
                scale=tanh_scale[branch],
            )

        def amplitude(step):
            nc.gpsimd.tensor_scalar(
                out=tanh["amp", step][:],
                in0=tanh["amp", step][:],
                scalar1=math.sqrt(2.0),
                scalar2=math.sqrt(2.0),
                op0=ALU.mult,
                op1=ALU.add,
            )

        ph_t = {}
        amp_t = {}
        half_cos = {}
        square = {}

        def turn_back(bank, source):
            for r in range(TILES):
                toks = slice(r * P, (r + 1) * P)
                nc.tensor.transpose(bank[:, toks], source[:, toks], ident[:])

        def phase_back(step):
            ph_t[step] = psum_ph.tile([P, CHUNK], F32, name="ph_t")
            turn_back(ph_t[step], tanh["ph", step])

        def sine(step):
            half_cos[step] = stage.tile([P, CHUNK], F32, name="half_cos")
            nc.scalar.activation(
                out=half_cos[step][:], in_=ph_t[step][:], func=ACT.Sin, bias=3.0 * math.pi / 8.0, scale=math.pi / 2.0
            )

        def square_half_cos(step, on_scalar):
            square[step] = stage.tile([P, CHUNK], F32, name="square")
            if on_scalar:
                nc.scalar.activation(out=square[step][:], in_=half_cos[step][:], func=ACT.Square)
            else:
                nc.vector.tensor_mul(out=square[step][:], in0=half_cos[step][:], in1=half_cos[step][:])

        def amp_back(step):
            amp_t[step] = psum_amp.tile([P, CHUNK], F32, name="amp_t")
            turn_back(amp_t[step], tanh["amp", step])

        def combine(step):
            c, j = divmod(step, BLOCKS)
            result = stage.tile([P, CHUNK], F32)
            nc.vector.scalar_tensor_tensor(
                out=result[:], in0=square[step][:], scalar=-0.5, in1=amp_t[step][:], op0=ALU.add, op1=ALU.mult
            )
            nc.sync.dma_start(out=out_blocks[c, j], in_=result[:].rearrange("p (r f) -> p r f", f=P))

        transpose_pair(0, psum_mx)
        copy_pair(0, False)
        transpose_pair(1, psum_mx)
        copy_pair(1, True)
        nc.vector.tensor_copy(out=bias_square[0 : 2 * BLOCKS, :], in_=bias_rows[:])
        bias_t = psum_x.tile([P, 2, 2, P], F32, tag="bank")
        nc.tensor.transpose(bias_t[:, 0, 0, :], bias_square[:], ident[:])
        warm_up(WARM_AFTER)
        group_weights("amp", 0)
        quantise_pair(0)
        quantise_weights("amp", 0)
        nc.vector.tensor_scalar_mul(out=bias["amp"][:], in0=bias_t[:, 0, 0, 0:BLOCKS], scalar1=0.5)
        nc.vector.tensor_copy(out=bias["ph"][:], in_=bias_t[:, 0, 0, BLOCKS : 2 * BLOCKS])
        quantise_pair(1)
        group_weights("ph", 0)
        group_weights("amp", 1)
        quantise_weights("ph", 0)
        group_weights("ph", 1)
        quantise_weights("amp", 1)

        pair_step = {2: 0, 3: 1}
        for e in range(4, PAIRS):
            pair_step[e] = 2 * e - X_LEAD
        pairs_at = {}
        for e in pair_step:
            pairs_at[pair_step[e]] = e

        for step in range(0, TAIL_FROM):
            if step % BLOCKS == 0 and step // BLOCKS + LOADS_AHEAD < CHUNKS:
                nc.sync.dma_start(out=x_all[:, step // BLOCKS + LOADS_AHEAD], in_=x_chunks[step // BLOCKS + LOADS_AHEAD])
            for branch in branches:
                multiply(step, branch)
            for branch in branches:
                squash(step, branch)
            amplitude(step)
            if step >= LAG_H:
                phase_back(step - LAG_H)
                sine(step - LAG_H)
            if step >= LAG_A:
                amp_back(step - LAG_A)
                combine(step - LAG_A)
            if step == 0:
                quantise_weights("ph", 1)
            if 1 <= step < BLOCKS - 1:
                for branch in branches:
                    group_weights(branch, step + 1)
                for branch in branches:
                    quantise_weights(branch, step + 1)
            if step in pairs_at:
                transpose_pair(pairs_at[step], psum_x)
                copy_pair(pairs_at[step], False)
            if step - 1 in pairs_at:
                quantise_pair(pairs_at[step - 1])
            if step >= LAG_H:
                square_half_cos(step - LAG_H, False)

        a, b = TAIL_FROM, TAIL_FROM + 1
        multiply(a, "ph")
        multiply(a, "amp")
        phase_back(a - 2)
        squash(a, "ph")
        sine(a - 2)
        squash(a, "amp")
        amplitude(a)
        amp_back(a - 4)
        combine(a - 4)
        square_half_cos(a - 2, False)
        phase_back(a - 1)
        multiply(b, "ph")
        multiply(b, "amp")
        sine(a - 1)
        squash(b, "ph")
        amp_back(a - 3)
        combine(a - 3)
        square_half_cos(a - 1, False)
        phase_back(a)
        sine(a)
        squash(b, "amp")
        amplitude(b)
        amp_back(a - 2)
        combine(a - 2)
        square_half_cos(a, False)
        phase_back(b)
        sine(b)
        amp_back(a - 1)
        combine(a - 1)
        square_half_cos(b, True)
        amp_back(a)
        combine(a)
        amp_back(b)
        combine(b)
